import numpy as np
import ml_dtypes


def mxq(x, axis, fmt="e4m3"):
    dtype, down = {"e4m3": (ml_dtypes.float8_e4m3fn, 7), "e5m2": (ml_dtypes.float8_e5m2, 14)}[fmt]
    v = np.moveaxis(np.asarray(x, np.float32).astype(ml_dtypes.bfloat16).astype(np.float64), axis, -1)
    blocks = v.reshape(v.shape[:-1] + (-1, 32))
    amax = np.abs(blocks).max(-1, keepdims=True)
    byte = np.maximum(np.where(amax > 0, np.frexp(amax)[1] - 1 + 127, 0) - down, 1)
    scale = np.exp2(byte - 127.0)
    codes = (blocks / scale).astype(np.float32).astype(dtype).astype(np.float64)
    return np.moveaxis((codes * scale).reshape(v.shape), -1, axis)


WIDE = False


def mx_kscale(k):
    if not WIDE:
        return np.ones(k)
    levels = np.array([10, -10, 5, -5, 0])
    a = np.random.permutation(np.resize(levels, k // 512 * 4)).reshape(k // 512, 4)
    idx = np.arange(k)
    return np.exp2(a[idx // 512, idx % 128 // 32])


BF16 = ml_dtypes.bfloat16


def bf(x):
    return np.asarray(x, np.float32).astype(BF16)


def f64(x):
    return np.asarray(x).astype(np.float64)


E2M1 = np.array([0.0, 0.5, 1.0, 1.5, 2.0, 3.0, 4.0, 6.0, -0.0, -0.5, -1.0, -1.5, -2.0, -3.0, -4.0, -6.0])


def pack_weight(w, fmt):
    k, n = w.shape
    w = f64(bf(w)).reshape(k // 32, 32, n)
    amax = np.abs(w).max(1)
    if fmt == "e4m3":
        byte = np.frexp(amax)[1] - 1 + 127 - 7
    else:
        mant, ex = np.frexp(amax / 6.0)
        byte = np.where(mant > 0.5, ex, ex - 1) + 127
    byte = np.clip(np.where(amax > 0, byte, 1), 1, 254)
    scaled = (w * np.exp2(127.0 - byte)[:, None, :]).reshape(k, n).astype(np.float32)
    by_word = np.ascontiguousarray(scaled.reshape(k // 512, 128, 4, n).transpose(0, 1, 3, 2))
    if fmt == "e4m3":
        words = by_word.astype(ml_dtypes.float8_e4m3fn).view(np.uint8)
    else:
        c = by_word.astype(ml_dtypes.float4_e2m1fn).view(np.uint8) & 0xF
        words = c[..., 0::2] | (c[..., 1::2] << 4)
    return np.ascontiguousarray(words), np.ascontiguousarray(byte.astype(np.uint8).reshape(k // 512, 16, n))


def unpack_weight(words, scales, fmt):
    g, p, n, _ = words.shape
    if fmt == "e4m3":
        vals = np.ascontiguousarray(words).view(ml_dtypes.float8_e4m3fn).astype(np.float64)
    else:
        nib = np.empty((g, p, n, 4), np.uint8)
        nib[..., 0::2] = words & 0xF
        nib[..., 1::2] = words >> 4
        vals = E2M1[nib]
    vals = vals * np.repeat(np.exp2(scales.astype(np.float64) - 127.0), 8, axis=1)[..., None]
    return vals.transpose(0, 1, 3, 2).reshape(g * 512, n)

def pack4(w):
    words, scales = pack_weight(w, "e2m1")
    return words.reshape(words.shape[0], 128, -1), scales


def unpack4(words, scales):
    return unpack_weight(words.reshape(words.shape[0], 128, -1, 2), scales, "e2m1")


B, S, D, BD, K = 8, 1024, 512, 512, 128
TS = 3.0


def sigmoid(v):
    return 1.0 / (1.0 + np.exp(-v))


def setup_inputs():
    s = mx_kscale(D)
    token_embeddings = bf(np.random.standard_normal((B, S, D)) * TS * s)
    splat_influences = bf(np.random.uniform(size=(B, S, K)))
    decoded = bf(np.random.standard_normal((B, K, D)) * 0.35)
    gate_W_words, gate_W_scales = pack4(np.random.standard_normal((D, D)) / (TS * np.sqrt(D)) / s[:, None])
    gate_b = bf(np.random.standard_normal(D) * 0.5)
    return {
        "token_embeddings": token_embeddings,
        "splat_influences": splat_influences,
        "decoded": decoded,
        "gate_W_words": gate_W_words,
        "gate_W_scales": gate_W_scales,
        "gate_b": gate_b,
    }


def reference(token_embeddings, splat_influences, decoded, gate_W_words, gate_W_scales, gate_b):
    flow = f64(splat_influences) @ f64(decoded)
    gate = sigmoid((mxq(f64(token_embeddings), 2, "e4m3") @ unpack4(gate_W_words, gate_W_scales)) + f64(gate_b))
    return flow * gate

@@ -1,0 +1,216 @@
+from contextlib import ExitStack
+
+import concourse.mybir as mybir
+from concourse.masks import make_identity
+
+F32 = mybir.dt.float32
+BF16 = mybir.dt.bfloat16
+I32 = mybir.dt.int32
+U32 = mybir.dt.uint32
+U8 = mybir.dt.uint8
+FP8X4 = mybir.dt.float8_e4m3fn_x4
+FP4X4 = mybir.dt.float4_e2m1fn_x4
+ALU = mybir.AluOpType
+ACT = mybir.ActivationFunctionType
+
+P = 128
+BATCHES = 8
+TOKENS = 1024
+D = 512
+SPLATS = 128
+TILES_PER_BATCH = TOKENS // P
+ROUND = 4
+ROUNDS_PER_BATCH = TILES_PER_BATCH // ROUND
+TILES = BATCHES * TILES_PER_BATCH
+ROUNDS = TILES // ROUND
+WORDS = D // 2
+PREPARE_AHEAD = 2
+LAG = 2
+
+FLOPS = 2 * BATCHES * TOKENS * D * D + 2 * BATCHES * TOKENS * SPLATS * D
+
+
+def tile_splatinformationflow_pb_t_kernel(
+    tc, token_embeddings, splat_influences, decoded, gate_W_words, gate_W_scales, gate_b, out
+):
+    nc = tc.nc
+    with ExitStack() as ctx:
+        consts = ctx.enter_context(tc.tile_pool(name="consts", bufs=1))
+        inputs = ctx.enter_context(tc.tile_pool(name="inputs", bufs=1))
+        prepared = ctx.enter_context(tc.tile_pool(name="prepared", bufs=PREPARE_AHEAD + 2))
+        work = ctx.enter_context(tc.tile_pool(name="work", bufs=6))
+        psum_x = ctx.enter_context(tc.psum_pool(name="psum_x", bufs=2))
+        psum_i = ctx.enter_context(tc.psum_pool(name="psum_i", bufs=1))
+        psum_acc = ctx.enter_context(tc.psum_pool(name="psum_acc", bufs=5))
+
+        ident_f32 = consts.tile([P, P], F32)
+        make_identity(nc, ident_f32[:])
+        ident_bf16 = consts.tile([P, P], BF16)
+        make_identity(nc, ident_bf16[:])
+
+        w_words = consts.tile([P, 2 * D], U8, align_bytes=64)
+        w_scales = consts.tile([P, D], U8, align_bytes=64)
+        nc.vector.memset(w_scales[:].bitcast(I32), 0)
+        bias = consts.tile([P, D], BF16)
+
+        x_sb = {}
+        infl_sb = {}
+        dec_sb = {}
+        x_t = {}
+        infl_t = {}
+        grouped = {}
+        codes = {}
+        code_scales = {}
+        infl_t_sb = {}
+        logits = {}
+        flow = {}
+        gate = {}
+        result = {}
+
+        ctx.enter_context(tc.manual_schedule())
+
+        def load_round(r):
+            b, half = divmod(r, ROUNDS_PER_BATCH)
+            x_sb[r] = inputs.tile([P, ROUND, D], BF16, name="x_sb", tag="x_sb", bufs=ROUNDS)
+            rows = token_embeddings[b].rearrange("(p t) d -> p t d", t=TILES_PER_BATCH)
+            nc.sync.dma_start(out=x_sb[r][:], in_=rows[:, half * ROUND : (half + 1) * ROUND, :])
+
+        def load_batch_small(b):
+            infl_sb[b] = inputs.tile(
+                [P, TILES_PER_BATCH, SPLATS], BF16, name="infl_sb", tag="infl_sb", bufs=BATCHES
+            )
+            nc.sync.dma_start(
+                out=infl_sb[b][:],
+                in_=splat_influences[b].rearrange("(p t) k -> p t k", t=TILES_PER_BATCH),
+            )
+            dec_sb[b] = inputs.tile([P, D], BF16, name="dec_sb", tag="dec_sb", bufs=BATCHES)
+            nc.sync.dma_start(out=dec_sb[b][:], in_=decoded[b])
+
+        def load_weight():
+            nc.sync.dma_start(out=w_words[:].bitcast(I32), in_=gate_W_words[0].bitcast(I32))
+            for quadrant in range(4):
+                nc.sync.dma_start(
+                    out=w_scales[32 * quadrant : 32 * quadrant + 4, :].bitcast(I32),
+                    in_=gate_W_scales[0, 4 * quadrant : 4 * quadrant + 4, :].bitcast(I32),
+                )
+            nc.sync.dma_start(out=bias[:], in_=gate_b.partition_broadcast(P))
+
+        def transpose_round(r):
+            for half in range(2):
+                x_t[r, half] = psum_x.tile([P, 2, 2, P], F32, name="x_t", tag="x_t")
+                for j in range(2):
+                    words = x_sb[r][:, 2 * half + j, :].bitcast(F32)
+                    for u in range(2):
+                        nc.tensor.transpose(
+                            x_t[r, half][:, j, u, :], words[:, u:WORDS:2], ident_f32[:]
+                        )
+            b, half_batch = divmod(r, ROUNDS_PER_BATCH)
+            infl_t[r] = psum_i.tile([P, ROUND, P], BF16, name="infl_t", tag="infl_t")
+            for j in range(ROUND):
+                nc.tensor.transpose(
+                    infl_t[r][:, j, :], infl_sb[b][:, half_batch * ROUND + j, :], ident_bf16[:]
+                )
+
+        def collect_round(r):
+            grouped[r] = prepared.tile(
+                [P, ROUND * P, 4], BF16, name="grouped", tag="grouped", bufs=2, align_bytes=64
+            )
+            pairs = (
+                grouped[r][:]
+                .rearrange("p s t -> p (s t)")
+                .bitcast(F32)
+                .rearrange("p (h j s u) -> p h j s u", h=2, j=2, u=2)
+            )
+            for half in range(2):
+                nc.scalar.copy(
+                    out=pairs[:, half], in_=x_t[r, half][:].rearrange("p j u s -> p j s u")
+                )
+            infl_t_sb[r] = prepared.tile([P, ROUND * P], BF16, name="infl_t_sb", tag="infl_t_sb")
+            nc.scalar.copy(out=infl_t_sb[r][:], in_=infl_t[r][:].rearrange("p j s -> p (j s)"))
+
+        def quantise_round(r):
+            codes[r] = prepared.tile([P, ROUND * P], U32, name="codes", tag="codes", align_bytes=64)
+            code_scales[r] = prepared.tile(
+                [P, ROUND * P], U8, name="code_scales", tag="code_scales", align_bytes=64
+            )
+            nc.vector.quantize_mx(
+                out=codes[r][:].bitcast(FP8X4),
+                scales=code_scales[r][:],
+                in_=grouped[r][:].rearrange("p s t -> p (s t)"),
+            )
+
+        def gate_matmul(t):
+            r, j = divmod(t, ROUND)
+            tokens = slice(j * P, (j + 1) * P)
+            logits[t] = psum_acc.tile([P, D], F32, name="logits", tag="acc")
+            nc.tensor.matmul_mx(
+                out=logits[t][:],
+                lhsT=codes[r][:, tokens].bitcast(FP8X4),
+                lhsT_scale=code_scales[r][:, tokens],
+                rhs=w_words[:].bitcast(FP4X4),
+                rhs_scale=w_scales[:],
+                start=True,
+                stop=True,
+            )
+
+        def flow_matmul(t):
+            r, j = divmod(t, ROUND)
+            flow[t] = psum_acc.tile([P, D], F32, name="flow", tag="acc")
+            nc.tensor.matmul(
+                out=flow[t][:],
+                lhsT=infl_t_sb[r][:, j * P : (j + 1) * P],
+                rhs=dec_sb[t // TILES_PER_BATCH][:],
+                start=True,
+                stop=True,
+            )
+
+        def gate_of(t):
+            gate[t] = work.tile([P, D], F32, name="gate", tag="gate")
+            nc.vector.tensor_tensor(out=gate[t][:], in0=logits[t][:], in1=bias[:], op=ALU.add)
+            nc.scalar.activation(out=gate[t][:], in_=gate[t][:], func=ACT.Sigmoid)
+
+        def product(t):
+            r, j = divmod(t, ROUND)
+            if j == 0:
+                result[r] = work.tile([P, ROUND, D], F32, name="result", tag="result")
+            nc.vector.tensor_tensor(
+                out=result[r][:, j, :], in0=flow[t][:], in1=gate[t][:], op=ALU.mult
+            )
+            if j == ROUND - 1:
+                b, half = divmod(r, ROUNDS_PER_BATCH)
+                rows = out[b].rearrange("(p t) d -> p t d", t=TILES_PER_BATCH)
+                nc.sync.dma_start(
+                    out=rows[:, half * ROUND : (half + 1) * ROUND, :], in_=result[r][:]
+                )
+
+        load_round(0)
+        load_batch_small(0)
+        load_weight()
+        load_round(1)
+        for b in range(1, BATCHES):
+            load_round(ROUNDS_PER_BATCH * b)
+            load_batch_small(b)
+            load_round(ROUNDS_PER_BATCH * b + 1)
+
+        for r in range(PREPARE_AHEAD):
+            transpose_round(r)
+            collect_round(r)
+            quantise_round(r)
+
+        for step in range(TILES + LAG):
+            ahead = step // ROUND + PREPARE_AHEAD
+            prepare = ahead < ROUNDS
+            if step < TILES:
+                gate_matmul(step)
+            if step >= LAG:
+                flow_matmul(step - LAG)
+            if prepare and step % ROUND == 0:
+                transpose_round(ahead)
+            if step < TILES:
+                gate_of(step)
+            if prepare and step % ROUND == 0:
+                collect_round(ahead)
+            if prepare and step % ROUND == ROUND - 1:
+                quantise_round(ahead)
+            if step >= LAG:
+                product(step - LAG)

@@ -26,6 +26,7 @@ ROUNDS = TILES // ROUND
 WORDS = D // 2
 PREPARE_AHEAD = 2
 LAG = 2
+GPSIMD_EVERY = 4
 
 FLOPS = 2 * BATCHES * TOKENS * D * D + 2 * BATCHES * TOKENS * SPLATS * D
 
@@ -173,9 +174,16 @@ def tile_splatinformationflow_pb_t_kernel(
             r, j = divmod(t, ROUND)
             if j == 0:
                 result[r] = work.tile([P, ROUND, D], F32, name="result", tag="result")
-            nc.vector.tensor_tensor(
-                out=result[r][:, j, :], in0=flow[t][:], in1=gate[t][:], op=ALU.mult
-            )
+            if t % GPSIMD_EVERY == 1:
+                flow_sb = work.tile([P, D], F32, name="flow_sb", tag="flow_sb", bufs=2)
+                nc.scalar.copy(out=flow_sb[:], in_=flow[t][:])
+                nc.gpsimd.tensor_tensor(
+                    out=result[r][:, j, :], in0=flow_sb[:], in1=gate[t][:], op=ALU.mult
+                )
+            else:
+                nc.vector.tensor_tensor(
+                    out=result[r][:, j, :], in0=flow[t][:], in1=gate[t][:], op=ALU.mult
+                )
             if j == ROUND - 1:
                 b, half = divmod(r, ROUNDS_PER_BATCH)
                 rows = out[b].rearrange("(p t) d -> p t d", t=TILES_PER_BATCH)

@@ -24,9 +24,10 @@ ROUNDS_PER_BATCH = TILES_PER_BATCH // ROUND
 TILES = BATCHES * TILES_PER_BATCH
 ROUNDS = TILES // ROUND
 WORDS = D // 2
-PREPARE_AHEAD = 2
+TRANSPOSE_AHEAD = 2
+QUANTISE_AHEAD = 1
 LAG = 2
-GPSIMD_EVERY = 4
+GPSIMD_EVERY = 3
 
 FLOPS = 2 * BATCHES * TOKENS * D * D + 2 * BATCHES * TOKENS * SPLATS * D
 
@@ -38,7 +39,7 @@ def tile_splatinformationflow_pb_t_kernel(
     with ExitStack() as ctx:
         consts = ctx.enter_context(tc.tile_pool(name="consts", bufs=1))
         inputs = ctx.enter_context(tc.tile_pool(name="inputs", bufs=1))
-        prepared = ctx.enter_context(tc.tile_pool(name="prepared", bufs=PREPARE_AHEAD + 2))
+        prepared = ctx.enter_context(tc.tile_pool(name="prepared", bufs=TRANSPOSE_AHEAD + 2))
         work = ctx.enter_context(tc.tile_pool(name="work", bufs=6))
         psum_x = ctx.enter_context(tc.psum_pool(name="psum_x", bufs=2))
         psum_i = ctx.enter_context(tc.psum_pool(name="psum_i", bufs=1))
@@ -174,7 +175,7 @@ def tile_splatinformationflow_pb_t_kernel(
             r, j = divmod(t, ROUND)
             if j == 0:
                 result[r] = work.tile([P, ROUND, D], F32, name="result", tag="result")
-            if t % GPSIMD_EVERY == 1:
+            if t % GPSIMD_EVERY == 0:
                 flow_sb = work.tile([P, D], F32, name="flow_sb", tag="flow_sb", bufs=2)
                 nc.scalar.copy(out=flow_sb[:], in_=flow[t][:])
                 nc.gpsimd.tensor_tensor(
@@ -184,41 +185,44 @@ def tile_splatinformationflow_pb_t_kernel(
                 nc.vector.tensor_tensor(
                     out=result[r][:, j, :], in0=flow[t][:], in1=gate[t][:], op=ALU.mult
                 )
-            if j == ROUND - 1:
-                b, half = divmod(r, ROUNDS_PER_BATCH)
-                rows = out[b].rearrange("(p t) d -> p t d", t=TILES_PER_BATCH)
+            b, half = divmod(r, ROUNDS_PER_BATCH)
+            rows = out[b].rearrange("(p t) d -> p t d", t=TILES_PER_BATCH)
+            if r == ROUNDS - 1:
+                nc.sync.dma_start(out=rows[:, half * ROUND + j, :], in_=result[r][:, j, :])
+            elif j == ROUND - 1:
                 nc.sync.dma_start(
                     out=rows[:, half * ROUND : (half + 1) * ROUND, :], in_=result[r][:]
                 )
 
         load_round(0)
         load_batch_small(0)
-        load_weight()
         load_round(1)
+        load_weight()
         for b in range(1, BATCHES):
             load_round(ROUNDS_PER_BATCH * b)
             load_batch_small(b)
             load_round(ROUNDS_PER_BATCH * b + 1)
 
-        for r in range(PREPARE_AHEAD):
-            transpose_round(r)
-            collect_round(r)
-            quantise_round(r)
+        transpose_round(0)
+        collect_round(0)
+        quantise_round(0)
+        transpose_round(1)
+        collect_round(1)
 
         for step in range(TILES + LAG):
-            ahead = step // ROUND + PREPARE_AHEAD
-            prepare = ahead < ROUNDS
+            r = step // ROUND
+            first = step % ROUND == 0
             if step < TILES:
                 gate_matmul(step)
             if step >= LAG:
                 flow_matmul(step - LAG)
-            if prepare and step % ROUND == 0:
-                transpose_round(ahead)
+            if first and r + TRANSPOSE_AHEAD < ROUNDS:
+                transpose_round(r + TRANSPOSE_AHEAD)
             if step < TILES:
                 gate_of(step)
-            if prepare and step % ROUND == 0:
-                collect_round(ahead)
-            if prepare and step % ROUND == ROUND - 1:
-                quantise_round(ahead)
+            if first and r + QUANTISE_AHEAD < ROUNDS:
+                quantise_round(r + QUANTISE_AHEAD)
+            if first and r + TRANSPOSE_AHEAD < ROUNDS:
+                collect_round(r + TRANSPOSE_AHEAD)
             if step >= LAG:
                 product(step - LAG)

@@ -20,6 +20,7 @@ D = 512
 SPLATS = 128
 TILES_PER_BATCH = TOKENS // P
 ROUND = 4
+PAIRS = ROUND // 2
 ROUNDS_PER_BATCH = TILES_PER_BATCH // ROUND
 TILES = BATCHES * TILES_PER_BATCH
 ROUNDS = TILES // ROUND
@@ -27,7 +28,9 @@ WORDS = D // 2
 TRANSPOSE_AHEAD = 2
 QUANTISE_AHEAD = 1
 LAG = 2
-GPSIMD_EVERY = 3
+GPSIMD_TILES = 2
+GPSIMD_OF = 5
+LAST_ON_VECTOR = 4
 
 FLOPS = 2 * BATCHES * TOKENS * D * D + 2 * BATCHES * TOKENS * SPLATS * D
 
@@ -66,6 +69,7 @@ def tile_splatinformationflow_pb_t_kernel(
         infl_t_sb = {}
         logits = {}
         flow = {}
+        flow_sb = {}
         gate = {}
         result = {}
 
@@ -98,22 +102,22 @@ def tile_splatinformationflow_pb_t_kernel(
             nc.sync.dma_start(out=bias[:], in_=gate_b.partition_broadcast(P))
 
         def transpose_round(r):
-            for half in range(2):
-                x_t[r, half] = psum_x.tile([P, 2, 2, P], F32, name="x_t", tag="x_t")
+            for pair in range(PAIRS):
+                x_t[r, pair] = psum_x.tile([P, 2, 2, P], F32, name="x_t", tag="x_t")
                 for j in range(2):
-                    words = x_sb[r][:, 2 * half + j, :].bitcast(F32)
+                    words = x_sb[r][:, 2 * pair + j, :].bitcast(F32)
                     for u in range(2):
                         nc.tensor.transpose(
-                            x_t[r, half][:, j, u, :], words[:, u:WORDS:2], ident_f32[:]
+                            x_t[r, pair][:, j, u, :], words[:, u:WORDS:2], ident_f32[:]
                         )
-            b, half_batch = divmod(r, ROUNDS_PER_BATCH)
+            b, part = divmod(r, ROUNDS_PER_BATCH)
             infl_t[r] = psum_i.tile([P, ROUND, P], BF16, name="infl_t", tag="infl_t")
             for j in range(ROUND):
                 nc.tensor.transpose(
-                    infl_t[r][:, j, :], infl_sb[b][:, half_batch * ROUND + j, :], ident_bf16[:]
+                    infl_t[r][:, j, :], infl_sb[b][:, part * ROUND + j, :], ident_bf16[:]
                 )
 
-        def collect_round(r):
+        def collect_round(r, vector_helps):
             grouped[r] = prepared.tile(
                 [P, ROUND * P, 4], BF16, name="grouped", tag="grouped", bufs=2, align_bytes=64
             )
@@ -121,12 +125,14 @@ def tile_splatinformationflow_pb_t_kernel(
                 grouped[r][:]
                 .rearrange("p s t -> p (s t)")
                 .bitcast(F32)
-                .rearrange("p (h j s u) -> p h j s u", h=2, j=2, u=2)
+                .rearrange("p (h j s u) -> p h j s u", h=PAIRS, j=2, u=2)
             )
-            for half in range(2):
-                nc.scalar.copy(
-                    out=pairs[:, half], in_=x_t[r, half][:].rearrange("p j u s -> p j s u")
-                )
+            for pair in range(PAIRS):
+                side_by_side = x_t[r, pair][:].rearrange("p j u s -> p j s u")
+                if vector_helps and pair == PAIRS - 1:
+                    nc.vector.tensor_copy(out=pairs[:, pair], in_=side_by_side)
+                else:
+                    nc.scalar.copy(out=pairs[:, pair], in_=side_by_side)
             infl_t_sb[r] = prepared.tile([P, ROUND * P], BF16, name="infl_t_sb", tag="infl_t_sb")
             nc.scalar.copy(out=infl_t_sb[r][:], in_=infl_t[r][:].rearrange("p j s -> p (j s)"))
 
@@ -171,15 +177,21 @@ def tile_splatinformationflow_pb_t_kernel(
             nc.vector.tensor_tensor(out=gate[t][:], in0=logits[t][:], in1=bias[:], op=ALU.add)
             nc.scalar.activation(out=gate[t][:], in_=gate[t][:], func=ACT.Sigmoid)
 
+        def on_gpsimd(t):
+            evenly_spread = (t * GPSIMD_TILES) % GPSIMD_OF < GPSIMD_TILES
+            return evenly_spread and t < TILES - LAST_ON_VECTOR
+
+        def flow_to_sbuf(t):
+            flow_sb[t] = work.tile([P, D], F32, name="flow_sb", tag="flow_sb", bufs=2)
+            nc.scalar.copy(out=flow_sb[t][:], in_=flow[t][:])
+
         def product(t):
             r, j = divmod(t, ROUND)
             if j == 0:
                 result[r] = work.tile([P, ROUND, D], F32, name="result", tag="result")
-            if t % GPSIMD_EVERY == 0:
-                flow_sb = work.tile([P, D], F32, name="flow_sb", tag="flow_sb", bufs=2)
-                nc.scalar.copy(out=flow_sb[:], in_=flow[t][:])
+            if on_gpsimd(t):
                 nc.gpsimd.tensor_tensor(
-                    out=result[r][:, j, :], in0=flow_sb[:], in1=gate[t][:], op=ALU.mult
+                    out=result[r][:, j, :], in0=flow_sb[t][:], in1=gate[t][:], op=ALU.mult
                 )
             else:
                 nc.vector.tensor_tensor(
@@ -187,27 +199,26 @@ def tile_splatinformationflow_pb_t_kernel(
                 )
             b, half = divmod(r, ROUNDS_PER_BATCH)
             rows = out[b].rearrange("(p t) d -> p t d", t=TILES_PER_BATCH)
-            if r == ROUNDS - 1:
+            if t >= TILES - LAST_ON_VECTOR:
                 nc.sync.dma_start(out=rows[:, half * ROUND + j, :], in_=result[r][:, j, :])
             elif j == ROUND - 1:
                 nc.sync.dma_start(
                     out=rows[:, half * ROUND : (half + 1) * ROUND, :], in_=result[r][:]
                 )
 
-        load_round(0)
-        load_batch_small(0)
-        load_round(1)
-        load_weight()
-        for b in range(1, BATCHES):
+        for b in range(BATCHES):
             load_round(ROUNDS_PER_BATCH * b)
             load_batch_small(b)
-            load_round(ROUNDS_PER_BATCH * b + 1)
+            for r in range(ROUNDS_PER_BATCH * b + 1, ROUNDS_PER_BATCH * (b + 1)):
+                load_round(r)
+                if r == 1:
+                    load_weight()
 
         transpose_round(0)
-        collect_round(0)
+        collect_round(0, vector_helps=True)
         quantise_round(0)
         transpose_round(1)
-        collect_round(1)
+        collect_round(1, vector_helps=True)
 
         for step in range(TILES + LAG):
             r = step // ROUND
@@ -218,11 +229,13 @@ def tile_splatinformationflow_pb_t_kernel(
                 flow_matmul(step - LAG)
             if first and r + TRANSPOSE_AHEAD < ROUNDS:
                 transpose_round(r + TRANSPOSE_AHEAD)
+            if step >= LAG and on_gpsimd(step - LAG):
+                flow_to_sbuf(step - LAG)
             if step < TILES:
                 gate_of(step)
             if first and r + QUANTISE_AHEAD < ROUNDS:
                 quantise_round(r + QUANTISE_AHEAD)
             if first and r + TRANSPOSE_AHEAD < ROUNDS:
-                collect_round(r + TRANSPOSE_AHEAD)
+                collect_round(r + TRANSPOSE_AHEAD, vector_helps=False)
             if step >= LAG:
                 product(step - LAG)

@@ -57,6 +57,8 @@ def tile_splatinformationflow_pb_t_kernel(
         w_scales = consts.tile([P, D], U8, align_bytes=64)
         nc.vector.memset(w_scales[:].bitcast(I32), 0)
         bias = consts.tile([P, D], BF16)
+        warm = consts.tile([P, 1], F32)
+        nc.vector.memset(warm[:], 0.0)
 
         x_sb = {}
         infl_sb = {}
@@ -74,6 +76,8 @@ def tile_splatinformationflow_pb_t_kernel(
         result = {}
 
         ctx.enter_context(tc.manual_schedule())
+
+        nc.scalar.activation(out=warm[:], in_=warm[:], func=ACT.Sigmoid)
 
         def load_round(r):
             b, half = divmod(r, ROUNDS_PER_BATCH)

@@ -48,6 +48,13 @@ def tile_splatinformationflow_pb_t_kernel(
         psum_i = ctx.enter_context(tc.psum_pool(name="psum_i", bufs=1))
         psum_acc = ctx.enter_context(tc.psum_pool(name="psum_acc", bufs=5))
 
+        bias_row = consts.tile([P, D], BF16)
+        nc.vector.memset(bias_row[:], 0.0)
+        nc.gpsimd.dma_start(out=bias_row[0:1, :], in_=gate_b.rearrange("(o d) -> o d", o=1))
+        ones = consts.tile([P, P], BF16)
+        nc.vector.memset(ones[:], 1.0)
+        bias = consts.tile([P, D], F32)
+
         ident_f32 = consts.tile([P, P], F32)
         make_identity(nc, ident_f32[:])
         ident_bf16 = consts.tile([P, P], BF16)
@@ -56,7 +63,6 @@ def tile_splatinformationflow_pb_t_kernel(
         w_words = consts.tile([P, 2 * D], U8, align_bytes=64)
         w_scales = consts.tile([P, D], U8, align_bytes=64)
         nc.vector.memset(w_scales[:].bitcast(I32), 0)
-        bias = consts.tile([P, D], BF16)
         warm = consts.tile([P, 1], F32)
         nc.vector.memset(warm[:], 0.0)
 
@@ -103,7 +109,6 @@ def tile_splatinformationflow_pb_t_kernel(
                     out=w_scales[32 * quadrant : 32 * quadrant + 4, :].bitcast(I32),
                     in_=gate_W_scales[0, 4 * quadrant : 4 * quadrant + 4, :].bitcast(I32),
                 )
-            nc.sync.dma_start(out=bias[:], in_=gate_b.partition_broadcast(P))
 
         def transpose_round(r):
             for pair in range(PAIRS):
@@ -221,6 +226,11 @@ def tile_splatinformationflow_pb_t_kernel(
         transpose_round(0)
         collect_round(0, vector_helps=True)
         quantise_round(0)
+        bias_everywhere = psum_acc.tile([P, D], F32, name="bias_everywhere", tag="acc")
+        nc.tensor.matmul(
+            out=bias_everywhere[:], lhsT=ones[:], rhs=bias_row[:], start=True, stop=True
+        )
+        nc.vector.tensor_copy(out=bias[:], in_=bias_everywhere[:])
         transpose_round(1)
         collect_round(1, vector_helps=True)
 

@@ -91,7 +91,7 @@ def tile_splatinformationflow_pb_t_kernel(
             rows = token_embeddings[b].rearrange("(p t) d -> p t d", t=TILES_PER_BATCH)
             nc.sync.dma_start(out=x_sb[r][:], in_=rows[:, half * ROUND : (half + 1) * ROUND, :])
 
-        def load_batch_small(b):
+        def load_influences(b):
             infl_sb[b] = inputs.tile(
                 [P, TILES_PER_BATCH, SPLATS], BF16, name="infl_sb", tag="infl_sb", bufs=BATCHES
             )
@@ -99,6 +99,8 @@ def tile_splatinformationflow_pb_t_kernel(
                 out=infl_sb[b][:],
                 in_=splat_influences[b].rearrange("(p t) k -> p t k", t=TILES_PER_BATCH),
             )
+
+        def load_decoded(b):
             dec_sb[b] = inputs.tile([P, D], BF16, name="dec_sb", tag="dec_sb", bufs=BATCHES)
             nc.sync.dma_start(out=dec_sb[b][:], in_=decoded[b])
 
@@ -217,11 +219,14 @@ def tile_splatinformationflow_pb_t_kernel(
 
         for b in range(BATCHES):
             load_round(ROUNDS_PER_BATCH * b)
-            load_batch_small(b)
+            load_influences(b)
+            if b == 0:
+                load_weight()
+                load_round(1)
+            load_decoded(b)
             for r in range(ROUNDS_PER_BATCH * b + 1, ROUNDS_PER_BATCH * (b + 1)):
-                load_round(r)
-                if r == 1:
-                    load_weight()
+                if r > 1:
+                    load_round(r)
 
         transpose_round(0)
         collect_round(0, vector_helps=True)

@@ -28,8 +28,7 @@ WORDS = D // 2
 TRANSPOSE_AHEAD = 2
 QUANTISE_AHEAD = 1
 LAG = 2
-GPSIMD_TILES = 2
-GPSIMD_OF = 5
+GPSIMD_TILES = (0, 4, 7)
 LAST_ON_VECTOR = 4
 
 FLOPS = 2 * BATCHES * TOKENS * D * D + 2 * BATCHES * TOKENS * SPLATS * D
@@ -189,8 +188,7 @@ def tile_splatinformationflow_pb_t_kernel(
             nc.scalar.activation(out=gate[t][:], in_=gate[t][:], func=ACT.Sigmoid)
 
         def on_gpsimd(t):
-            evenly_spread = (t * GPSIMD_TILES) % GPSIMD_OF < GPSIMD_TILES
-            return evenly_spread and t < TILES - LAST_ON_VECTOR
+            return t % (2 * ROUND) in GPSIMD_TILES and t < TILES - LAST_ON_VECTOR
 
         def flow_to_sbuf(t):
             flow_sb[t] = work.tile([P, D], F32, name="flow_sb", tag="flow_sb", bufs=2)

@@ -28,7 +28,7 @@ WORDS = D // 2
 TRANSPOSE_AHEAD = 2
 QUANTISE_AHEAD = 1
 LAG = 2
-GPSIMD_TILES = (0, 4, 7)
+GPSIMD_TILES = (2, 5, 6)
 LAST_ON_VECTOR = 4
 
 FLOPS = 2 * BATCHES * TOKENS * D * D + 2 * BATCHES * TOKENS * SPLATS * D

@@ -25,10 +25,7 @@ ROUNDS_PER_BATCH = TILES_PER_BATCH // ROUND
 TILES = BATCHES * TILES_PER_BATCH
 ROUNDS = TILES // ROUND
 WORDS = D // 2
-TRANSPOSE_AHEAD = 2
-QUANTISE_AHEAD = 1
 LAG = 2
-GPSIMD_TILES = (2, 5, 6)
 LAST_ON_VECTOR = 4
 
 FLOPS = 2 * BATCHES * TOKENS * D * D + 2 * BATCHES * TOKENS * SPLATS * D
@@ -41,7 +38,7 @@ def tile_splatinformationflow_pb_t_kernel(
     with ExitStack() as ctx:
         consts = ctx.enter_context(tc.tile_pool(name="consts", bufs=1))
         inputs = ctx.enter_context(tc.tile_pool(name="inputs", bufs=1))
-        prepared = ctx.enter_context(tc.tile_pool(name="prepared", bufs=TRANSPOSE_AHEAD + 2))
+        prepared = ctx.enter_context(tc.tile_pool(name="prepared", bufs=4))
         work = ctx.enter_context(tc.tile_pool(name="work", bufs=6))
         psum_x = ctx.enter_context(tc.psum_pool(name="psum_x", bufs=2))
         psum_i = ctx.enter_context(tc.psum_pool(name="psum_i", bufs=1))
@@ -111,15 +108,16 @@ def tile_splatinformationflow_pb_t_kernel(
                     in_=gate_W_scales[0, 4 * quadrant : 4 * quadrant + 4, :].bitcast(I32),
                 )
 
-        def transpose_round(r):
-            for pair in range(PAIRS):
-                x_t[r, pair] = psum_x.tile([P, 2, 2, P], F32, name="x_t", tag="x_t")
-                for j in range(2):
-                    words = x_sb[r][:, 2 * pair + j, :].bitcast(F32)
-                    for u in range(2):
-                        nc.tensor.transpose(
-                            x_t[r, pair][:, j, u, :], words[:, u:WORDS:2], ident_f32[:]
-                        )
+        def transpose_tokens(r, pair):
+            x_t[r, pair] = psum_x.tile([P, 2, 2, P], F32, name="x_t", tag="x_t")
+            for j in range(2):
+                words = x_sb[r][:, 2 * pair + j, :].bitcast(F32)
+                for u in range(2):
+                    nc.tensor.transpose(
+                        x_t[r, pair][:, j, u, :], words[:, u:WORDS:2], ident_f32[:]
+                    )
+
+        def transpose_influences(r):
             b, part = divmod(r, ROUNDS_PER_BATCH)
             infl_t[r] = psum_i.tile([P, ROUND, P], BF16, name="infl_t", tag="infl_t")
             for j in range(ROUND):
@@ -127,22 +125,20 @@ def tile_splatinformationflow_pb_t_kernel(
                     infl_t[r][:, j, :], infl_sb[b][:, part * ROUND + j, :], ident_bf16[:]
                 )
 
-        def collect_round(r, vector_helps):
-            grouped[r] = prepared.tile(
-                [P, ROUND * P, 4], BF16, name="grouped", tag="grouped", bufs=2, align_bytes=64
-            )
+        def collect_tokens(r, pair, copy):
+            if pair == 0:
+                grouped[r] = prepared.tile(
+                    [P, ROUND * P, 4], BF16, name="grouped", tag="grouped", bufs=2, align_bytes=64
+                )
             pairs = (
                 grouped[r][:]
                 .rearrange("p s t -> p (s t)")
                 .bitcast(F32)
                 .rearrange("p (h j s u) -> p h j s u", h=PAIRS, j=2, u=2)
             )
-            for pair in range(PAIRS):
-                side_by_side = x_t[r, pair][:].rearrange("p j u s -> p j s u")
-                if vector_helps and pair == PAIRS - 1:
-                    nc.vector.tensor_copy(out=pairs[:, pair], in_=side_by_side)
-                else:
-                    nc.scalar.copy(out=pairs[:, pair], in_=side_by_side)
+            copy(out=pairs[:, pair], in_=x_t[r, pair][:].rearrange("p j u s -> p j s u"))
+
+        def collect_influences(r):
             infl_t_sb[r] = prepared.tile([P, ROUND * P], BF16, name="infl_t_sb", tag="infl_t_sb")
             nc.scalar.copy(out=infl_t_sb[r][:], in_=infl_t[r][:].rearrange("p j s -> p (j s)"))
 
@@ -183,12 +179,16 @@ def tile_splatinformationflow_pb_t_kernel(
             )
 
         def gate_of(t):
-            gate[t] = work.tile([P, D], F32, name="gate", tag="gate")
-            nc.vector.tensor_tensor(out=gate[t][:], in0=logits[t][:], in1=bias[:], op=ALU.add)
-            nc.scalar.activation(out=gate[t][:], in_=gate[t][:], func=ACT.Sigmoid)
+            biased = work.tile([P, D], F32, name="biased", tag="biased")
+            nc.vector.tensor_tensor(out=biased[:], in0=logits[t][:], in1=bias[:], op=ALU.add)
+            if on_gpsimd(t):
+                gate[t] = work.tile([P, D], F32, name="gate_g", tag="gate_g", bufs=4)
+            else:
+                gate[t] = work.tile([P, D], F32, name="gate", tag="gate")
+            nc.scalar.activation(out=gate[t][:], in_=biased[:], func=ACT.Sigmoid)
 
         def on_gpsimd(t):
-            return t % (2 * ROUND) in GPSIMD_TILES and t < TILES - LAST_ON_VECTOR
+            return (t % ROUND == 0 or t % (3 * ROUND) == 6) and t < TILES - 4
 
         def flow_to_sbuf(t):
             flow_sb[t] = work.tile([P, D], F32, name="flow_sb", tag="flow_sb", bufs=2)
@@ -208,7 +208,7 @@ def tile_splatinformationflow_pb_t_kernel(
                 )
             b, half = divmod(r, ROUNDS_PER_BATCH)
             rows = out[b].rearrange("(p t) d -> p t d", t=TILES_PER_BATCH)
-            if t >= TILES - LAST_ON_VECTOR:
+            if t >= TILES - 4:
                 nc.sync.dma_start(out=rows[:, half * ROUND + j, :], in_=result[r][:, j, :])
             elif j == ROUND - 1:
                 nc.sync.dma_start(
@@ -226,33 +226,62 @@ def tile_splatinformationflow_pb_t_kernel(
                 if r > 1:
                     load_round(r)
 
-        transpose_round(0)
-        collect_round(0, vector_helps=True)
+        transpose_tokens(0, 0)
+        transpose_tokens(0, 1)
+        collect_tokens(0, 0, nc.scalar.copy)
+        collect_tokens(0, 1, nc.vector.tensor_copy)
+        transpose_influences(0)
+        collect_influences(0)
         quantise_round(0)
         bias_everywhere = psum_acc.tile([P, D], F32, name="bias_everywhere", tag="acc")
         nc.tensor.matmul(
             out=bias_everywhere[:], lhsT=ones[:], rhs=bias_row[:], start=True, stop=True
         )
         nc.vector.tensor_copy(out=bias[:], in_=bias_everywhere[:])
-        transpose_round(1)
-        collect_round(1, vector_helps=True)
 
+        def due(step, ahead):
+            r, rest = divmod(step + ahead, ROUND)
+            return r if rest == 0 and 1 <= r < ROUNDS else None
+
+        def prepare_transposes(step):
+            r = due(step, 7)
+            if r is not None:
+                transpose_influences(r)
+            r = due(step, 6)
+            if r is not None:
+                transpose_tokens(r, 0)
+            r = due(step, 5)
+            if r is not None:
+                transpose_tokens(r, 1)
+
+        def prepare_collects(step):
+            r = due(step, 7)
+            if r is not None:
+                collect_influences(r)
+            r = due(step, 5)
+            if r is not None:
+                collect_tokens(r, 0, nc.scalar.copy)
+            r = due(step, 5)
+            if r is not None:
+                collect_tokens(r, 1, nc.scalar.copy)
+
+        for step in range(-3, 0):
+            prepare_transposes(step)
+            prepare_collects(step)
         for step in range(TILES + LAG):
-            r = step // ROUND
-            first = step % ROUND == 0
             if step < TILES:
                 gate_matmul(step)
             if step >= LAG:
                 flow_matmul(step - LAG)
-            if first and r + TRANSPOSE_AHEAD < ROUNDS:
-                transpose_round(r + TRANSPOSE_AHEAD)
+            if step < TILES:
+                prepare_transposes(step)
             if step >= LAG and on_gpsimd(step - LAG):
                 flow_to_sbuf(step - LAG)
+            prepare_collects(step)
             if step < TILES:
                 gate_of(step)
-            if first and r + QUANTISE_AHEAD < ROUNDS:
-                quantise_round(r + QUANTISE_AHEAD)
-            if first and r + TRANSPOSE_AHEAD < ROUNDS:
-                collect_round(r + TRANSPOSE_AHEAD, vector_helps=False)
+            r = due(step, 3)
+            if r is not None:
+                quantise_round(r)
             if step >= LAG:
                 product(step - LAG)

@@ -28,6 +28,8 @@ WORDS = D // 2
 LAG = 2
 LAST_ON_VECTOR = 4
 
+GROUP = 1
+
 FLOPS = 2 * BATCHES * TOKENS * D * D + 2 * BATCHES * TOKENS * SPLATS * D
 
 
@@ -39,7 +41,7 @@ def tile_splatinformationflow_pb_t_kernel(
         consts = ctx.enter_context(tc.tile_pool(name="consts", bufs=1))
         inputs = ctx.enter_context(tc.tile_pool(name="inputs", bufs=1))
         prepared = ctx.enter_context(tc.tile_pool(name="prepared", bufs=4))
-        work = ctx.enter_context(tc.tile_pool(name="work", bufs=6))
+        work = ctx.enter_context(tc.tile_pool(name="work", bufs=2))
         psum_x = ctx.enter_context(tc.psum_pool(name="psum_x", bufs=2))
         psum_i = ctx.enter_context(tc.psum_pool(name="psum_i", bufs=1))
         psum_acc = ctx.enter_context(tc.psum_pool(name="psum_acc", bufs=5))
@@ -74,8 +76,8 @@ def tile_splatinformationflow_pb_t_kernel(
         logits = {}
         flow = {}
         flow_sb = {}
+        biased = {}
         gate = {}
-        result = {}
 
         ctx.enter_context(tc.manual_schedule())
 
@@ -178,41 +180,46 @@ def tile_splatinformationflow_pb_t_kernel(
                 stop=True,
             )
 
-        def gate_of(t):
-            biased = work.tile([P, D], F32, name="biased", tag="biased")
-            nc.vector.tensor_tensor(out=biased[:], in0=logits[t][:], in1=bias[:], op=ALU.add)
-            if on_gpsimd(t):
-                gate[t] = work.tile([P, D], F32, name="gate_g", tag="gate_g", bufs=4)
-            else:
-                gate[t] = work.tile([P, D], F32, name="gate", tag="gate")
-            nc.scalar.activation(out=gate[t][:], in_=biased[:], func=ACT.Sigmoid)
+        def biased_of(t):
+            group, i = divmod(t, GROUP)
+            if i == 0:
+                biased[group] = work.tile([P, GROUP, D], F32, name="biased", tag="biased", bufs=6)
+            nc.vector.tensor_tensor(
+                out=biased[group][:, i, :], in0=logits[t][:], in1=bias[:], op=ALU.add
+            )
+
+        def gates_of(first, count):
+            r, j = divmod(first, ROUND)
+            if j == 0:
+                gate[r] = work.tile([P, ROUND, D], F32, name="gate", tag="gate", bufs=6)
+            i = first % GROUP
+            nc.scalar.activation(
+                out=gate[r][:, j : j + count, :],
+                in_=biased[first // GROUP][:, i : i + count, :],
+                func=ACT.Sigmoid,
+            )
 
         def on_gpsimd(t):
-            return (t % ROUND == 0 or t % (3 * ROUND) == 6) and t < TILES - 4
+            return (t % 8 in (0, 4, 7)) and t < TILES - LAST_ON_VECTOR
 
         def flow_to_sbuf(t):
-            flow_sb[t] = work.tile([P, D], F32, name="flow_sb", tag="flow_sb", bufs=2)
+            flow_sb[t] = work.tile([P, D], F32, name="flow_sb", tag="flow_sb", bufs=3)
             nc.scalar.copy(out=flow_sb[t][:], in_=flow[t][:])
 
         def product(t):
             r, j = divmod(t, ROUND)
-            if j == 0:
-                result[r] = work.tile([P, ROUND, D], F32, name="result", tag="result")
+            out_tile = gate[r][:, j, :]
             if on_gpsimd(t):
-                nc.gpsimd.tensor_tensor(
-                    out=result[r][:, j, :], in0=flow_sb[t][:], in1=gate[t][:], op=ALU.mult
-                )
+                nc.gpsimd.tensor_tensor(out=out_tile, in0=flow_sb[t][:], in1=out_tile, op=ALU.mult)
             else:
-                nc.vector.tensor_tensor(
-                    out=result[r][:, j, :], in0=flow[t][:], in1=gate[t][:], op=ALU.mult
-                )
+                nc.vector.tensor_tensor(out=out_tile, in0=flow[t][:], in1=out_tile, op=ALU.mult)
             b, half = divmod(r, ROUNDS_PER_BATCH)
             rows = out[b].rearrange("(p t) d -> p t d", t=TILES_PER_BATCH)
             if t >= TILES - 4:
-                nc.sync.dma_start(out=rows[:, half * ROUND + j, :], in_=result[r][:, j, :])
+                nc.sync.dma_start(out=rows[:, half * ROUND + j, :], in_=gate[r][:, j, :])
             elif j == ROUND - 1:
                 nc.sync.dma_start(
-                    out=rows[:, half * ROUND : (half + 1) * ROUND, :], in_=result[r][:]
+                    out=rows[:, half * ROUND : (half + 1) * ROUND, :], in_=gate[r][:]
                 )
 
         for b in range(BATCHES):
@@ -244,18 +251,18 @@ def tile_splatinformationflow_pb_t_kernel(
             return r if rest == 0 and 1 <= r < ROUNDS else None
 
         def prepare_transposes(step):
-            r = due(step, 7)
-            if r is not None:
-                transpose_influences(r)
             r = due(step, 6)
             if r is not None:
-                transpose_tokens(r, 0)
+                transpose_influences(r)
             r = due(step, 5)
+            if r is not None:
+                transpose_tokens(r, 0)
+            r = due(step, 6)
             if r is not None:
                 transpose_tokens(r, 1)
 
         def prepare_collects(step):
-            r = due(step, 7)
+            r = due(step, 6)
             if r is not None:
                 collect_influences(r)
             r = due(step, 5)
@@ -263,23 +270,33 @@ def tile_splatinformationflow_pb_t_kernel(
                 collect_tokens(r, 0, nc.scalar.copy)
             r = due(step, 5)
             if r is not None:
-                collect_tokens(r, 1, nc.scalar.copy)
+                collect_tokens(r, 1, nc.vector.tensor_copy if r == 1 and True else nc.scalar.copy)
 
-        for step in range(-3, 0):
-            prepare_transposes(step)
-            prepare_collects(step)
-        for step in range(TILES + LAG):
-            if step < TILES:
+        START = -4
+        GFLOW = LAG - 0
+        GCOPY = LAG - 0
+        for step in range(START, TILES + LAG):
+            if 0 <= step < TILES:
                 gate_matmul(step)
-            if step >= LAG:
-                flow_matmul(step - LAG)
+            t = step - GFLOW
+            if 0 <= t < TILES and on_gpsimd(t):
+                flow_matmul(t)
+            t = step - LAG + 0
+            if 0 <= t < TILES and not on_gpsimd(t):
+                flow_matmul(t)
             if step < TILES:
                 prepare_transposes(step)
-            if step >= LAG and on_gpsimd(step - LAG):
-                flow_to_sbuf(step - LAG)
+            if 0 <= step < TILES:
+                biased_of(step)
             prepare_collects(step)
-            if step < TILES:
-                gate_of(step)
+            t = step - GCOPY
+            if 0 <= t < TILES and on_gpsimd(t):
+                flow_to_sbuf(t)
+            if 0 <= step < TILES:
+                if step >= TILES - 4:
+                    gates_of(step, 1)
+                elif step % GROUP == GROUP - 1:
+                    gates_of(step - GROUP + 1, GROUP)
             r = due(step, 3)
             if r is not None:
                 quantise_round(r)

@@ -200,7 +200,7 @@ def tile_splatinformationflow_pb_t_kernel(
             )
 
         def on_gpsimd(t):
-            return (t % 8 in (0, 4, 7)) and t < TILES - LAST_ON_VECTOR
+            return (t % 8 in (0, 4, 7) or t == 58) and t < TILES - LAST_ON_VECTOR
 
         def flow_to_sbuf(t):
             flow_sb[t] = work.tile([P, D], F32, name="flow_sb", tag="flow_sb", bufs=3)
@@ -215,12 +215,14 @@ def tile_splatinformationflow_pb_t_kernel(
                 nc.vector.tensor_tensor(out=out_tile, in0=flow[t][:], in1=out_tile, op=ALU.mult)
             b, half = divmod(r, ROUNDS_PER_BATCH)
             rows = out[b].rearrange("(p t) d -> p t d", t=TILES_PER_BATCH)
-            if t >= TILES - 4:
-                nc.sync.dma_start(out=rows[:, half * ROUND + j, :], in_=gate[r][:, j, :])
-            elif j == ROUND - 1:
-                nc.sync.dma_start(
-                    out=rows[:, half * ROUND : (half + 1) * ROUND, :], in_=gate[r][:]
-                )
+            count = 1 if t >= TILES - 12 else ROUND
+            if (j + 1) % count == 0:
+                tiles = slice(j + 1 - count, j + 1)
+                for cols in [slice(0, D)]:
+                    nc.sync.dma_start(
+                        out=rows[:, half * ROUND + tiles.start : half * ROUND + tiles.stop, cols],
+                        in_=gate[r][:, tiles, cols],
+                    )
 
         for b in range(BATCHES):
             load_round(ROUNDS_PER_BATCH * b)

@@ -200,7 +200,7 @@ def tile_splatinformationflow_pb_t_kernel(
             )
 
         def on_gpsimd(t):
-            return (t % 8 in (0, 4, 7) or t == 58) and t < TILES - LAST_ON_VECTOR
+            return (t % 8 in (0, 4, 7)) and t < TILES - LAST_ON_VECTOR
 
         def flow_to_sbuf(t):
             flow_sb[t] = work.tile([P, D], F32, name="flow_sb", tag="flow_sb", bufs=3)

@@ -25,10 +25,15 @@ ROUNDS_PER_BATCH = TILES_PER_BATCH // ROUND
 TILES = BATCHES * TILES_PER_BATCH
 ROUNDS = TILES // ROUND
 WORDS = D // 2
-LAG = 2
-LAST_ON_VECTOR = 4
 
-GROUP = 1
+LAG = 3
+TRANSPOSE_PAIR = (7, 5)
+COLLECT_PAIR = (6, 5)
+QUANTISE = 3
+INFLUENCES = 4
+
+LAST_ON_VECTOR = 7
+STORED_ALONE = 12
 
 FLOPS = 2 * BATCHES * TOKENS * D * D + 2 * BATCHES * TOKENS * SPLATS * D
 
@@ -41,10 +46,9 @@ def tile_splatinformationflow_pb_t_kernel(
         consts = ctx.enter_context(tc.tile_pool(name="consts", bufs=1))
         inputs = ctx.enter_context(tc.tile_pool(name="inputs", bufs=1))
         prepared = ctx.enter_context(tc.tile_pool(name="prepared", bufs=4))
-        work = ctx.enter_context(tc.tile_pool(name="work", bufs=2))
+        work = ctx.enter_context(tc.tile_pool(name="work", bufs=6))
         psum_x = ctx.enter_context(tc.psum_pool(name="psum_x", bufs=2))
-        psum_i = ctx.enter_context(tc.psum_pool(name="psum_i", bufs=1))
-        psum_acc = ctx.enter_context(tc.psum_pool(name="psum_acc", bufs=5))
+        psum_acc = ctx.enter_context(tc.psum_pool(name="psum_acc", bufs=6))
 
         bias_row = consts.tile([P, D], BF16)
         nc.vector.memset(bias_row[:], 0.0)
@@ -119,13 +123,10 @@ def tile_splatinformationflow_pb_t_kernel(
                         x_t[r, pair][:, j, u, :], words[:, u:WORDS:2], ident_f32[:]
                     )
 
-        def transpose_influences(r):
-            b, part = divmod(r, ROUNDS_PER_BATCH)
-            infl_t[r] = psum_i.tile([P, ROUND, P], BF16, name="infl_t", tag="infl_t")
-            for j in range(ROUND):
-                nc.tensor.transpose(
-                    infl_t[r][:, j, :], infl_sb[b][:, part * ROUND + j, :], ident_bf16[:]
-                )
+        def transpose_influences(b):
+            infl_t[b] = psum_acc.tile([P, TILES_PER_BATCH, P], BF16, name="infl_t", tag="acc")
+            for j in range(TILES_PER_BATCH):
+                nc.tensor.transpose(infl_t[b][:, j, :], infl_sb[b][:, j, :], ident_bf16[:])
 
         def collect_tokens(r, pair, copy):
             if pair == 0:
@@ -140,9 +141,11 @@ def tile_splatinformationflow_pb_t_kernel(
             )
             copy(out=pairs[:, pair], in_=x_t[r, pair][:].rearrange("p j u s -> p j s u"))
 
-        def collect_influences(r):
-            infl_t_sb[r] = prepared.tile([P, ROUND * P], BF16, name="infl_t_sb", tag="infl_t_sb")
-            nc.scalar.copy(out=infl_t_sb[r][:], in_=infl_t[r][:].rearrange("p j s -> p (j s)"))
+        def collect_influences(b):
+            infl_t_sb[b] = prepared.tile(
+                [P, TILES_PER_BATCH * P], BF16, name="infl_t_sb", tag="infl_t_sb", bufs=3
+            )
+            nc.scalar.copy(out=infl_t_sb[b][:], in_=infl_t[b][:].rearrange("p j s -> p (j s)"))
 
         def quantise_round(r):
             codes[r] = prepared.tile([P, ROUND * P], U32, name="codes", tag="codes", align_bytes=64)
@@ -170,59 +173,48 @@ def tile_splatinformationflow_pb_t_kernel(
             )
 
         def flow_matmul(t):
-            r, j = divmod(t, ROUND)
+            b, j = divmod(t, TILES_PER_BATCH)
             flow[t] = psum_acc.tile([P, D], F32, name="flow", tag="acc")
             nc.tensor.matmul(
                 out=flow[t][:],
-                lhsT=infl_t_sb[r][:, j * P : (j + 1) * P],
-                rhs=dec_sb[t // TILES_PER_BATCH][:],
+                lhsT=infl_t_sb[b][:, j * P : (j + 1) * P],
+                rhs=dec_sb[b][:],
                 start=True,
                 stop=True,
             )
 
-        def biased_of(t):
-            group, i = divmod(t, GROUP)
-            if i == 0:
-                biased[group] = work.tile([P, GROUP, D], F32, name="biased", tag="biased", bufs=6)
-            nc.vector.tensor_tensor(
-                out=biased[group][:, i, :], in0=logits[t][:], in1=bias[:], op=ALU.add
-            )
+        def add_bias(t):
+            biased[t] = work.tile([P, D], F32, name="biased", tag="biased")
+            nc.vector.tensor_tensor(out=biased[t][:], in0=logits[t][:], in1=bias[:], op=ALU.add)
 
-        def gates_of(first, count):
-            r, j = divmod(first, ROUND)
+        def gate_of(t):
+            r, j = divmod(t, ROUND)
             if j == 0:
-                gate[r] = work.tile([P, ROUND, D], F32, name="gate", tag="gate", bufs=6)
-            i = first % GROUP
-            nc.scalar.activation(
-                out=gate[r][:, j : j + count, :],
-                in_=biased[first // GROUP][:, i : i + count, :],
-                func=ACT.Sigmoid,
-            )
+                gate[r] = work.tile([P, ROUND, D], F32, name="gate", tag="gate")
+            nc.scalar.activation(out=gate[r][:, j, :], in_=biased[t][:], func=ACT.Sigmoid)
 
         def on_gpsimd(t):
-            return (t % 8 in (0, 4, 7)) and t < TILES - LAST_ON_VECTOR
+            return (t % ROUND == 2 or t % (3 * ROUND) == 7) and t < TILES - LAST_ON_VECTOR
 
         def flow_to_sbuf(t):
-            flow_sb[t] = work.tile([P, D], F32, name="flow_sb", tag="flow_sb", bufs=3)
+            flow_sb[t] = work.tile([P, D], F32, name="flow_sb", tag="flow_sb", bufs=4)
             nc.scalar.copy(out=flow_sb[t][:], in_=flow[t][:])
 
         def product(t):
             r, j = divmod(t, ROUND)
-            out_tile = gate[r][:, j, :]
+            output = gate[r][:, j, :]
             if on_gpsimd(t):
-                nc.gpsimd.tensor_tensor(out=out_tile, in0=flow_sb[t][:], in1=out_tile, op=ALU.mult)
+                nc.gpsimd.tensor_tensor(out=output, in0=flow_sb[t][:], in1=output, op=ALU.mult)
             else:
-                nc.vector.tensor_tensor(out=out_tile, in0=flow[t][:], in1=out_tile, op=ALU.mult)
+                nc.vector.tensor_tensor(out=output, in0=flow[t][:], in1=output, op=ALU.mult)
             b, half = divmod(r, ROUNDS_PER_BATCH)
             rows = out[b].rearrange("(p t) d -> p t d", t=TILES_PER_BATCH)
-            count = 1 if t >= TILES - 12 else ROUND
-            if (j + 1) % count == 0:
-                tiles = slice(j + 1 - count, j + 1)
-                for cols in [slice(0, D)]:
-                    nc.sync.dma_start(
-                        out=rows[:, half * ROUND + tiles.start : half * ROUND + tiles.stop, cols],
-                        in_=gate[r][:, tiles, cols],
-                    )
+            if t >= TILES - STORED_ALONE:
+                nc.sync.dma_start(out=rows[:, half * ROUND + j, :], in_=output)
+            elif j == ROUND - 1:
+                nc.sync.dma_start(
+                    out=rows[:, half * ROUND : (half + 1) * ROUND, :], in_=gate[r][:]
+                )
 
         for b in range(BATCHES):
             load_round(ROUNDS_PER_BATCH * b)
@@ -231,9 +223,8 @@ def tile_splatinformationflow_pb_t_kernel(
                 load_weight()
                 load_round(1)
             load_decoded(b)
-            for r in range(ROUNDS_PER_BATCH * b + 1, ROUNDS_PER_BATCH * (b + 1)):
-                if r > 1:
-                    load_round(r)
+            if b > 0:
+                load_round(ROUNDS_PER_BATCH * b + 1)
 
         transpose_tokens(0, 0)
         transpose_tokens(0, 1)
@@ -248,59 +239,45 @@ def tile_splatinformationflow_pb_t_kernel(
         )
         nc.vector.tensor_copy(out=bias[:], in_=bias_everywhere[:])
 
-        def due(step, ahead):
+        def due_round(step, ahead):
             r, rest = divmod(step + ahead, ROUND)
             return r if rest == 0 and 1 <= r < ROUNDS else None
 
-        def prepare_transposes(step):
-            r = due(step, 6)
-            if r is not None:
-                transpose_influences(r)
-            r = due(step, 5)
-            if r is not None:
-                transpose_tokens(r, 0)
-            r = due(step, 6)
-            if r is not None:
-                transpose_tokens(r, 1)
+        def due_batch(step, ahead):
+            b, rest = divmod(step + ahead, TILES_PER_BATCH)
+            return b if rest == 0 and 1 <= b < BATCHES else None
 
-        def prepare_collects(step):
-            r = due(step, 6)
-            if r is not None:
-                collect_influences(r)
-            r = due(step, 5)
-            if r is not None:
-                collect_tokens(r, 0, nc.scalar.copy)
-            r = due(step, 5)
-            if r is not None:
-                collect_tokens(r, 1, nc.vector.tensor_copy if r == 1 and True else nc.scalar.copy)
+        for step in range(ROUND - max(TRANSPOSE_PAIR), TILES + LAG):
+            has_tile = 0 <= step < TILES
+            done = step - LAG
 
-        START = -4
-        GFLOW = LAG - 0
-        GCOPY = LAG - 0
-        for step in range(START, TILES + LAG):
-            if 0 <= step < TILES:
+            if done >= 0:
+                flow_matmul(done)
+            if has_tile:
                 gate_matmul(step)
-            t = step - GFLOW
-            if 0 <= t < TILES and on_gpsimd(t):
-                flow_matmul(t)
-            t = step - LAG + 0
-            if 0 <= t < TILES and not on_gpsimd(t):
-                flow_matmul(t)
-            if step < TILES:
-                prepare_transposes(step)
-            if 0 <= step < TILES:
-                biased_of(step)
-            prepare_collects(step)
-            t = step - GCOPY
-            if 0 <= t < TILES and on_gpsimd(t):
-                flow_to_sbuf(t)
-            if 0 <= step < TILES:
-                if step >= TILES - 4:
-                    gates_of(step, 1)
-                elif step % GROUP == GROUP - 1:
-                    gates_of(step - GROUP + 1, GROUP)
-            r = due(step, 3)
+            b = due_batch(step, INFLUENCES)
+            if b is not None:
+                transpose_influences(b)
+            for pair in range(PAIRS):
+                r = due_round(step, TRANSPOSE_PAIR[pair])
+                if r is not None:
+                    transpose_tokens(r, pair)
+
+            if has_tile:
+                add_bias(step)
+            if done >= 0 and on_gpsimd(done):
+                flow_to_sbuf(done)
+            b = due_batch(step, INFLUENCES)
+            if b is not None:
+                collect_influences(b)
+            for pair in range(PAIRS):
+                r = due_round(step, COLLECT_PAIR[pair])
+                if r is not None:
+                    collect_tokens(r, pair, nc.scalar.copy)
+            if has_tile:
+                gate_of(step)
+            r = due_round(step, QUANTISE)
             if r is not None:
                 quantise_round(r)
-            if step >= LAG:
-                product(step - LAG)
+            if done >= 0:
+                product(done)

@@ -218,9 +218,10 @@ def tile_splatinformationflow_pb_t_kernel(
 
         for b in range(BATCHES):
             load_round(ROUNDS_PER_BATCH * b)
-            load_influences(b)
             if b == 0:
                 load_weight()
+            load_influences(b)
+            if b == 0:
                 load_round(1)
             load_decoded(b)
             if b > 0:

from contextlib import ExitStack

import concourse.mybir as mybir
from concourse.masks import make_identity

F32 = mybir.dt.float32
BF16 = mybir.dt.bfloat16
I32 = mybir.dt.int32
U32 = mybir.dt.uint32
U8 = mybir.dt.uint8
FP8X4 = mybir.dt.float8_e4m3fn_x4
FP4X4 = mybir.dt.float4_e2m1fn_x4
ALU = mybir.AluOpType
ACT = mybir.ActivationFunctionType

P = 128
BATCHES = 8
TOKENS = 1024
D = 512
SPLATS = 128
TILES_PER_BATCH = TOKENS // P
ROUND = 4
PAIRS = ROUND // 2
ROUNDS_PER_BATCH = TILES_PER_BATCH // ROUND
TILES = BATCHES * TILES_PER_BATCH
ROUNDS = TILES // ROUND
WORDS = D // 2

LAG = 3
TRANSPOSE_PAIR = (7, 5)
COLLECT_PAIR = (6, 5)
QUANTISE = 3
INFLUENCES = 4

LAST_ON_VECTOR = 7
STORED_ALONE = 12

FLOPS = 2 * BATCHES * TOKENS * D * D + 2 * BATCHES * TOKENS * SPLATS * D


def tile_splatinformationflow_pb_t_kernel(
    tc, token_embeddings, splat_influences, decoded, gate_W_words, gate_W_scales, gate_b, out
):
    nc = tc.nc
    with ExitStack() as ctx:
        consts = ctx.enter_context(tc.tile_pool(name="consts", bufs=1))
        inputs = ctx.enter_context(tc.tile_pool(name="inputs", bufs=1))
        prepared = ctx.enter_context(tc.tile_pool(name="prepared", bufs=4))
        work = ctx.enter_context(tc.tile_pool(name="work", bufs=6))
        psum_x = ctx.enter_context(tc.psum_pool(name="psum_x", bufs=2))
        psum_acc = ctx.enter_context(tc.psum_pool(name="psum_acc", bufs=6))

        bias_row = consts.tile([P, D], BF16)
        nc.vector.memset(bias_row[:], 0.0)
        nc.gpsimd.dma_start(out=bias_row[0:1, :], in_=gate_b.rearrange("(o d) -> o d", o=1))
        ones = consts.tile([P, P], BF16)
        nc.vector.memset(ones[:], 1.0)
        bias = consts.tile([P, D], F32)

        ident_f32 = consts.tile([P, P], F32)
        make_identity(nc, ident_f32[:])
        ident_bf16 = consts.tile([P, P], BF16)
        make_identity(nc, ident_bf16[:])

        w_words = consts.tile([P, 2 * D], U8, align_bytes=64)
        w_scales = consts.tile([P, D], U8, align_bytes=64)
        nc.vector.memset(w_scales[:].bitcast(I32), 0)
        warm = consts.tile([P, 1], F32)
        nc.vector.memset(warm[:], 0.0)

        x_sb = {}
        infl_sb = {}
        dec_sb = {}
        x_t = {}
        infl_t = {}
        grouped = {}
        codes = {}
        code_scales = {}
        infl_t_sb = {}
        logits = {}
        flow = {}
        flow_sb = {}
        biased = {}
        gate = {}

        ctx.enter_context(tc.manual_schedule())

        nc.scalar.activation(out=warm[:], in_=warm[:], func=ACT.Sigmoid)

        def load_round(r):
            b, half = divmod(r, ROUNDS_PER_BATCH)
            x_sb[r] = inputs.tile([P, ROUND, D], BF16, name="x_sb", tag="x_sb", bufs=ROUNDS)
            rows = token_embeddings[b].rearrange("(p t) d -> p t d", t=TILES_PER_BATCH)
            nc.sync.dma_start(out=x_sb[r][:], in_=rows[:, half * ROUND : (half + 1) * ROUND, :])

        def load_influences(b):
            infl_sb[b] = inputs.tile(
                [P, TILES_PER_BATCH, SPLATS], BF16, name="infl_sb", tag="infl_sb", bufs=BATCHES
            )
            nc.sync.dma_start(
                out=infl_sb[b][:],
                in_=splat_influences[b].rearrange("(p t) k -> p t k", t=TILES_PER_BATCH),
            )

        def load_decoded(b):
            dec_sb[b] = inputs.tile([P, D], BF16, name="dec_sb", tag="dec_sb", bufs=BATCHES)
            nc.sync.dma_start(out=dec_sb[b][:], in_=decoded[b])

        def load_weight():
            nc.sync.dma_start(out=w_words[:].bitcast(I32), in_=gate_W_words[0].bitcast(I32))
            for quadrant in range(4):
                nc.sync.dma_start(
                    out=w_scales[32 * quadrant : 32 * quadrant + 4, :].bitcast(I32),
                    in_=gate_W_scales[0, 4 * quadrant : 4 * quadrant + 4, :].bitcast(I32),
                )

        def transpose_tokens(r, pair):
            x_t[r, pair] = psum_x.tile([P, 2, 2, P], F32, name="x_t", tag="x_t")
            for j in range(2):
                words = x_sb[r][:, 2 * pair + j, :].bitcast(F32)
                for u in range(2):
                    nc.tensor.transpose(
                        x_t[r, pair][:, j, u, :], words[:, u:WORDS:2], ident_f32[:]
                    )

        def transpose_influences(b):
            infl_t[b] = psum_acc.tile([P, TILES_PER_BATCH, P], BF16, name="infl_t", tag="acc")
            for j in range(TILES_PER_BATCH):
                nc.tensor.transpose(infl_t[b][:, j, :], infl_sb[b][:, j, :], ident_bf16[:])

        def collect_tokens(r, pair, copy):
            if pair == 0:
                grouped[r] = prepared.tile(
                    [P, ROUND * P, 4], BF16, name="grouped", tag="grouped", bufs=2, align_bytes=64
                )
            pairs = (
                grouped[r][:]
                .rearrange("p s t -> p (s t)")
                .bitcast(F32)
                .rearrange("p (h j s u) -> p h j s u", h=PAIRS, j=2, u=2)
            )
            copy(out=pairs[:, pair], in_=x_t[r, pair][:].rearrange("p j u s -> p j s u"))

        def collect_influences(b):
            infl_t_sb[b] = prepared.tile(
                [P, TILES_PER_BATCH * P], BF16, name="infl_t_sb", tag="infl_t_sb", bufs=3
            )
            nc.scalar.copy(out=infl_t_sb[b][:], in_=infl_t[b][:].rearrange("p j s -> p (j s)"))

        def quantise_round(r):
            codes[r] = prepared.tile([P, ROUND * P], U32, name="codes", tag="codes", align_bytes=64)
            code_scales[r] = prepared.tile(
                [P, ROUND * P], U8, name="code_scales", tag="code_scales", align_bytes=64
            )
            nc.vector.quantize_mx(
                out=codes[r][:].bitcast(FP8X4),
                scales=code_scales[r][:],
                in_=grouped[r][:].rearrange("p s t -> p (s t)"),
            )

        def gate_matmul(t):
            r, j = divmod(t, ROUND)
            tokens = slice(j * P, (j + 1) * P)
            logits[t] = psum_acc.tile([P, D], F32, name="logits", tag="acc")
            nc.tensor.matmul_mx(
                out=logits[t][:],
                lhsT=codes[r][:, tokens].bitcast(FP8X4),
                lhsT_scale=code_scales[r][:, tokens],
                rhs=w_words[:].bitcast(FP4X4),
                rhs_scale=w_scales[:],
                start=True,
                stop=True,
            )

        def flow_matmul(t):
            b, j = divmod(t, TILES_PER_BATCH)
            flow[t] = psum_acc.tile([P, D], F32, name="flow", tag="acc")
            nc.tensor.matmul(
                out=flow[t][:],
                lhsT=infl_t_sb[b][:, j * P : (j + 1) * P],
                rhs=dec_sb[b][:],
                start=True,
                stop=True,
            )

        def add_bias(t):
            biased[t] = work.tile([P, D], F32, name="biased", tag="biased")
            nc.vector.tensor_tensor(out=biased[t][:], in0=logits[t][:], in1=bias[:], op=ALU.add)

        def gate_of(t):
            r, j = divmod(t, ROUND)
            if j == 0:
                gate[r] = work.tile([P, ROUND, D], F32, name="gate", tag="gate")
            nc.scalar.activation(out=gate[r][:, j, :], in_=biased[t][:], func=ACT.Sigmoid)

        def on_gpsimd(t):
            return (t % ROUND == 2 or t % (3 * ROUND) == 7) and t < TILES - LAST_ON_VECTOR

        def flow_to_sbuf(t):
            flow_sb[t] = work.tile([P, D], F32, name="flow_sb", tag="flow_sb", bufs=4)
            nc.scalar.copy(out=flow_sb[t][:], in_=flow[t][:])

        def product(t):
            r, j = divmod(t, ROUND)
            output = gate[r][:, j, :]
            if on_gpsimd(t):
                nc.gpsimd.tensor_tensor(out=output, in0=flow_sb[t][:], in1=output, op=ALU.mult)
            else:
                nc.vector.tensor_tensor(out=output, in0=flow[t][:], in1=output, op=ALU.mult)
            b, half = divmod(r, ROUNDS_PER_BATCH)
            rows = out[b].rearrange("(p t) d -> p t d", t=TILES_PER_BATCH)
            if t >= TILES - STORED_ALONE:
                nc.sync.dma_start(out=rows[:, half * ROUND + j, :], in_=output)
            elif j == ROUND - 1:
                nc.sync.dma_start(
                    out=rows[:, half * ROUND : (half + 1) * ROUND, :], in_=gate[r][:]
                )

        for b in range(BATCHES):
            load_round(ROUNDS_PER_BATCH * b)
            if b == 0:
                load_weight()
            load_influences(b)
            if b == 0:
                load_round(1)
            load_decoded(b)
            if b > 0:
                load_round(ROUNDS_PER_BATCH * b + 1)

        transpose_tokens(0, 0)
        transpose_tokens(0, 1)
        collect_tokens(0, 0, nc.scalar.copy)
        collect_tokens(0, 1, nc.vector.tensor_copy)
        transpose_influences(0)
        collect_influences(0)
        quantise_round(0)
        bias_everywhere = psum_acc.tile([P, D], F32, name="bias_everywhere", tag="acc")
        nc.tensor.matmul(
            out=bias_everywhere[:], lhsT=ones[:], rhs=bias_row[:], start=True, stop=True
        )
        nc.vector.tensor_copy(out=bias[:], in_=bias_everywhere[:])

        def due_round(step, ahead):
            r, rest = divmod(step + ahead, ROUND)
            return r if rest == 0 and 1 <= r < ROUNDS else None

        def due_batch(step, ahead):
            b, rest = divmod(step + ahead, TILES_PER_BATCH)
            return b if rest == 0 and 1 <= b < BATCHES else None

        for step in range(ROUND - max(TRANSPOSE_PAIR), TILES + LAG):
            has_tile = 0 <= step < TILES
            done = step - LAG

            if done >= 0:
                flow_matmul(done)
            if has_tile:
                gate_matmul(step)
            b = due_batch(step, INFLUENCES)
            if b is not None:
                transpose_influences(b)
            for pair in range(PAIRS):
                r = due_round(step, TRANSPOSE_PAIR[pair])
                if r is not None:
                    transpose_tokens(r, pair)

            if has_tile:
                add_bias(step)
            if done >= 0 and on_gpsimd(done):
                flow_to_sbuf(done)
            b = due_batch(step, INFLUENCES)
            if b is not None:
                collect_influences(b)
            for pair in range(PAIRS):
                r = due_round(step, COLLECT_PAIR[pair])
                if r is not None:
                    collect_tokens(r, pair, nc.scalar.copy)
            if has_tile:
                gate_of(step)
            r = due_round(step, QUANTISE)
            if r is not None:
                quantise_round(r)
            if done >= 0:
                product(done)
